import numpy as np
import ml_dtypes


def mxq(x, axis, fmt="e4m3"):
    dtype, down = {"e4m3": (ml_dtypes.float8_e4m3fn, 7), "e5m2": (ml_dtypes.float8_e5m2, 14)}[fmt]
    v = np.moveaxis(np.asarray(x, np.float32).astype(ml_dtypes.bfloat16).astype(np.float64), axis, -1)
    blocks = v.reshape(v.shape[:-1] + (-1, 32))
    amax = np.abs(blocks).max(-1, keepdims=True)
    byte = np.maximum(np.where(amax > 0, np.frexp(amax)[1] - 1 + 127, 0) - down, 1)
    scale = np.exp2(byte - 127.0)
    codes = (blocks / scale).astype(np.float32).astype(dtype).astype(np.float64)
    return np.moveaxis((codes * scale).reshape(v.shape), -1, axis)


WIDE = False


def mx_kscale(k):
    if not WIDE:
        return np.ones(k)
    levels = np.array([10, -10, 5, -5, 0])
    if k % 512:
        return np.exp2(np.random.permutation(np.resize(levels, k // 32))).repeat(32)
    a = np.empty((k // 512, 16))
    for p in range(k // 512):
        a[p, :8] = np.random.permutation(np.resize(levels, 8))
        for g in range(8):
            far = levels[np.abs(levels - a[p, g]) >= 10]
            a[p, g + 8] = far[np.random.randint(len(far))]
    return np.exp2(a.ravel()).repeat(32)


BF16 = ml_dtypes.bfloat16


def bf(x):
    return np.asarray(x, np.float32).astype(BF16)


def f64(x):
    return np.asarray(x).astype(np.float64)


B, T, C, CO, HS, DW, DA, DV, DG = 4, 128, 2048, 2048, 64, 128, 128, 128, 256


def sigmoid(u):
    return 1.0 / (1.0 + np.exp(-u))


def setup_inputs():
    n = np.random.standard_normal
    s = mx_kscale(C)
    return {
        "x": bf(n((B, T, C)) * s),
        "x_v": bf(n((1, 1, C)) * 0.3),
        "W_v": bf(n((CO, C)) / np.sqrt(C) / s),
        "v_hid": bf(n((B, T, DV))),
        "v2": bf(n((DV, CO)) / np.sqrt(DV)),
        "v0": bf(0.73 + n((1, 1, CO)) * 0.2),
        "v_first": bf(n((B, T, CO))),
    }


def reference(x, x_v, W_v, v_hid, v2, v0, v_first):
    x = f64(x)
    prev = np.concatenate([np.zeros_like(x[:, :1]), x[:, :-1]], axis=1)
    xv = x + (prev - x) * f64(x_v)
    v = mxq(xv, 2, "e4m3") @ mxq(f64(W_v), 1, "e4m3").T
    mix = sigmoid(f64(v0) + f64(v_hid) @ f64(v2))
    return v + (f64(v_first) - v) * mix

@@ -1,0 +1,293 @@
+from contextlib import ExitStack
+
+import concourse.mybir as mybir
+from concourse.masks import make_identity
+
+F32 = mybir.dt.float32
+BF16 = mybir.dt.bfloat16
+U32 = mybir.dt.uint32
+U8 = mybir.dt.uint8
+FP8X4 = mybir.dt.float8_e4m3fn_x4
+ALU = mybir.AluOpType
+ACT = mybir.ActivationFunctionType
+
+P = 128
+NB = 4
+NT = NB * P
+C = 2048
+CO = 2048
+NG = 4
+CW = 512
+NCH = CO // CW
+
+FLOPS = 2 * NT * C * CO + 2 * NT * 128 * CO
+
+PINNED = True
+REG_ENG = "V"
+T1_ENG = "G"
+
+
+def tile_full_tmix_params_pb_kernel(tc, x, x_v, W_v, v_hid, v2, v0, v_first, out):
+    nc = tc.nc
+    with ExitStack() as ctx:
+        if PINNED:
+            ctx.enter_context(tc.manual_schedule())
+        const = ctx.enter_context(tc.tile_pool(name="const", bufs=1))
+        wraw_pool = ctx.enter_context(tc.tile_pool(name="wraw", bufs=6))
+        wg_pool = ctx.enter_context(tc.tile_pool(name="wg", bufs=3))
+        wc_pool = ctx.enter_context(tc.tile_pool(name="wc", bufs=6))
+        xw_pool = ctx.enter_context(tc.tile_pool(name="xw", bufs=2))
+        vf_pool = ctx.enter_context(tc.tile_pool(name="vf", bufs=3))
+        p_pool = ctx.enter_context(tc.tile_pool(name="pp", bufs=4))
+        acc_pool = ctx.enter_context(tc.psum_pool(name="acc", bufs=4))
+        tp_pool = ctx.enter_context(tc.psum_pool(name="tp", bufs=4))
+
+        ident_f = const.tile([P, P], F32, name="ident_f")
+        make_identity(nc, ident_f[:])
+        ident_b = const.tile([P, P], BF16, name="ident_b")
+        make_identity(nc, ident_b[:])
+        v0rows = const.tile([P, P], BF16, name="v0rows")
+        nc.gpsimd.memset(v0rows[:], 0.0)
+
+        a_bf = const.tile([P, 4, 4], BF16, name="a_bf")
+        nc.scalar.dma_start(out=a_bf[:], in_=x_v.rearrange("a b c -> (a b c)").rearrange("(m p e) -> p m e", p=P, e=4))
+
+        warm = const.tile([P, 1], F32, name="warm")
+        nc.vector.memset(warm[:], 0.0)
+        nc.scalar.activation(out=warm[:], in_=warm[:], func=ACT.Sigmoid)
+
+        x_tbk = x.rearrange("b t k -> t b k")
+        w_units = W_v.rearrange("(n r p) k -> n p r k", r=2, p=P)
+        vf_chunks = v_first.rearrange("b t (c n) -> c t b n", n=CW)
+        xp = [const.tile([P, NB, C // NG], BF16, name="xp%d" % g) for g in range(NG)]
+        vh_sb = const.tile([P, NB, P], BF16, name="vh_sb")
+        v2_sb = const.tile([P, CO], BF16, name="v2_sb")
+        wraw = {}
+        vf_sb = {}
+
+        def load_w(n):
+            wraw[n] = wraw_pool.tile([P, 2, C], BF16, name="wr")
+            nc.sync.dma_start(out=wraw[n][:], in_=w_units[n])
+
+        def load_vf(c):
+            vf_sb[c] = vf_pool.tile([P, NB, CW], BF16, name="vf")
+            nc.sync.dma_start(out=vf_sb[c][:], in_=vf_chunks[c])
+
+        def load_x(g):
+            nc.sync.dma_start(out=xp[g][:], in_=x_tbk[:, :, 512 * g:512 * g + 512])
+
+        load_x(0)
+        nc.sync.dma_start(out=vh_sb[:], in_=v_hid.rearrange("b t d -> t b d"))
+        nc.sync.dma_start(out=v0rows[0:16, :], in_=v0.rearrange("a b c -> (a b c)").rearrange("(j p) -> j p", p=P))
+        nc.sync.dma_start(out=v2_sb[:], in_=v2)
+        load_x(1)
+        load_w(0)
+        load_w(1)
+        load_x(2)
+        load_x(3)
+        load_vf(0)
+        load_w(2)
+        load_w(3)
+        load_vf(1)
+        load_w(4)
+        load_w(5)
+        load_vf(2)
+        load_vf(3)
+        load_w(6)
+        load_w(7)
+
+        a32 = const.tile([P, 16], F32, name="a32")
+        nc.vector.tensor_copy(out=a32[:], in_=a_bf[:].rearrange("p m e -> p (m e)"))
+        oma32 = const.tile([P, 16], F32, name="oma32")
+        nc.vector.tensor_scalar(out=oma32[:], in0=a32[:], scalar1=-1.0, scalar2=1.0, op0=ALU.mult, op1=ALU.add)
+
+        xcodes = const.tile([P, NG, NT], U32, name="xcodes", align_bytes=64)
+        xscales = const.tile([P, NG, NT], U8, name="xscales", align_bytes=64)
+        mix = {}
+        t1 = {}
+        for c in range(NCH):
+            for i in range(NB):
+                mix[(c, i)] = const.tile([P, CW], F32, name="mix%d_%d" % (c, i))
+                t1[(c, i)] = const.tile([P, CW], F32, name="t1_%d_%d" % (c, i))
+        vhT = const.tile([P, NT], BF16, name="vhT")
+        v0c = const.tile([P, 16], F32, name="v0c")
+
+        xbanks = {}
+        y0s = {}
+        xvps = {}
+        xgs = {}
+
+        def x_transposes(j):
+            g, u = divmod(j, 2)
+            bank = tp_pool.tile([P, NT], F32, name="xbank", tag="tp")
+            for b in range(NB):
+                nc.tensor.transpose(bank[:, P * b:P * b + P], xp[g][:, b, :].bitcast(F32)[:, u:2 * P:2], ident_f[:])
+            xbanks[j] = bank
+
+        def x_scale(j):
+            g, u = divmod(j, 2)
+            if u == 0:
+                y0s[g] = xw_pool.tile([P, 4, NT], F32, name="y0")
+            view = xbanks[j][:].bitcast(BF16).rearrange("p (s e) -> p s e", e=2)
+            for e in range(2):
+                t = 2 * u + e
+                nc.scalar.activation(out=y0s[g][:, t, :], in_=view[:, :, e], func=ACT.Copy,
+                                     scale=oma32[:, 4 * g + t:4 * g + t + 1])
+
+        def x_add(j):
+            g, u = divmod(j, 2)
+            if u == 0:
+                xvps[g] = xw_pool.tile([P, 4, NT], BF16, name="xvp")
+            y0v = y0s[g][:].rearrange("p t (b s) -> p t b s", b=NB)
+            xvv = xvps[g][:].rearrange("p t (b s) -> p t b s", b=NB)
+            view = xbanks[j][:].bitcast(BF16).rearrange("p (b s e) -> p b s e", b=NB, e=2)
+            for e in range(2):
+                t = 2 * u + e
+                nc.vector.scalar_tensor_tensor(out=xvv[:, t, :, 1:P], in0=view[:, :, 0:P - 1, e],
+                                               scalar=a32[:, 4 * g + t:4 * g + t + 1], in1=y0v[:, t, :, 1:P],
+                                               op0=ALU.mult, op1=ALU.add)
+
+        def x_regroup(g):
+            y0v = y0s[g][:].rearrange("p t (b s) -> p t b s", b=NB)
+            xvv = xvps[g][:].rearrange("p t (b s) -> p t b s", b=NB)
+            nc.vector.tensor_copy(out=xvv[:, :, :, 0], in_=y0v[:, :, :, 0])
+            xgs[g] = xw_pool.tile([P, NT * 4], BF16, name="xg", align_bytes=64)
+            dst = xgs[g][:].rearrange("p (c i t) -> p c t i", i=4, t=4)
+            src = xvps[g][:].rearrange("p t (c i) -> p c t i", i=4)
+            nc.vector.tensor_copy(out=dst, in_=src)
+
+        def x_quant(g):
+            nc.vector.quantize_mx(out=xcodes[:, g, :].bitcast(FP8X4), scales=xscales[:, g, :], in_=xgs[g][:])
+
+        def gate_setup():
+            bank = tp_pool.tile([P, NT], BF16, name="vhbank", tag="tp")
+            for b in range(NB):
+                nc.tensor.transpose(bank[:, P * b:P * b + P], vh_sb[:, b, :], ident_b[:])
+            nc.scalar.copy(out=vhT[:], in_=bank[:])
+            vbank = tp_pool.tile([P, P], BF16, name="vbank", tag="tp")
+            nc.tensor.transpose(vbank[:], v0rows[:], ident_b[:])
+            nc.vector.tensor_copy(out=v0c[:], in_=vbank[:, 0:16])
+
+        hps = {}
+
+        def gate_mm(k):
+            c, i = divmod(k, NB)
+            hp = tp_pool.tile([P, CW], F32, name="hp", tag="tp")
+            nc.tensor.matmul(out=hp[:], lhsT=vhT[:, P * i:P * i + P], rhs=v2_sb[:, CW * c:CW * c + CW],
+                             start=True, stop=False)
+            for q in range(4):
+                jj = 4 * c + q
+                nc.tensor.matmul(out=hp[:, P * q:P * q + P], lhsT=v0c[:, jj:jj + 1].to_broadcast([P, P]),
+                                 rhs=ident_f[:], is_transpose=True, start=False, stop=(q == 3))
+            hps[k] = hp
+
+        def gate_sig(k):
+            nc.scalar.activation(out=mix[divmod(k, NB)][:], in_=hps[k][:], func=ACT.Sigmoid)
+
+        def first_term(k, eng):
+            c, i = divmod(k, NB)
+            eng.tensor_tensor(out=t1[(c, i)][:], in0=vf_sb[c][:, i, :], in1=mix[(c, i)][:], op=ALU.mult)
+
+        wbanks = {}
+        wgs = {}
+        wcs = {}
+
+        def w_transposes(b):
+            c, rest = divmod(b, 8)
+            g, h = divmod(rest, 2)
+            bank = tp_pool.tile([P, 512], F32, name="wbank", tag="tp")
+            for u in range(2):
+                for r in range(2):
+                    lo = 256 * g + u
+                    nc.tensor.transpose(bank[:, 256 * u + P * r:256 * u + P * r + P],
+                                        wraw[2 * c + h][:, r, :].bitcast(F32)[:, lo:256 * g + 256:2], ident_f[:])
+            wbanks[b] = bank
+
+        def w_copy(b):
+            k, h = divmod(b, 2)
+            if h == 0:
+                wgs[k] = wg_pool.tile([P, CW * 4], BF16, name="wg", align_bytes=64)
+            nc.scalar.copy(out=wgs[k][:].bitcast(F32)[:, 512 * h:512 * h + 512].rearrange("p (c u) -> p c u", u=2),
+                           in_=wbanks[b][:].rearrange("p (u c) -> p c u", u=2))
+
+        def w_quant(k):
+            wc = wc_pool.tile([P, CW], U32, name="wc", align_bytes=64)
+            ws = wc_pool.tile([P, CW], U8, name="ws", align_bytes=64)
+            nc.vector.quantize_mx(out=wc[:].bitcast(FP8X4), scales=ws[:], in_=wgs[k][:])
+            wcs[k] = (wc, ws)
+
+        accs = {}
+
+        def mx(s):
+            todo = sorted([((s - i) % NG, i) for i in range(NB) if 0 <= s - i < 16], reverse=True)
+            for g, i in todo:
+                c = (s - i) // NG
+                wc, ws = wcs[s - i]
+                if g == 0:
+                    accs[(c, i)] = acc_pool.tile([P, CW], F32, name="acc", tag="acc")
+                nc.tensor.matmul_mx(out=accs[(c, i)][:],
+                                    lhsT=xcodes[:, g, P * i:P * i + P].bitcast(FP8X4),
+                                    lhsT_scale=xscales[:, g, P * i:P * i + P],
+                                    rhs=wc[:].bitcast(FP8X4), rhs_scale=ws[:],
+                                    start=(g == 0), stop=(g == NG - 1))
+
+        pts = {}
+
+        def second_term(c, i):
+            pts[(c, i)] = p_pool.tile([P, CW], F32, name="pt")
+            nc.vector.scalar_tensor_tensor(out=pts[(c, i)][:], in0=mix[(c, i)][:], scalar=1.0, in1=accs[(c, i)][:],
+                                           op0=ALU.subtract, op1=ALU.mult)
+
+        def finish(c, i, eng):
+            eng.tensor_tensor(out=t1[(c, i)][:], in0=t1[(c, i)][:], in1=pts[(c, i)][:], op=ALU.subtract)
+            nc.sync.dma_start(out=out[i, :, CW * c:CW * c + CW], in_=t1[(c, i)][:])
+
+        x_transposes(0)
+        gate_setup()
+        for j in range(10):
+            g, u = divmod(j, 2)
+            b = j - 2
+            if j < 8:
+                x_scale(j)
+                gate_mm(j)
+                x_add(j)
+                gate_sig(j)
+            if 0 <= b < 8:
+                w_transposes(b)
+            if j < 7:
+                x_transposes(j + 1)
+            if 0 <= b < 8:
+                w_copy(b)
+            if j < 8 and u == 1:
+                x_regroup(g)
+            if u == 0 and 1 <= g <= 4:
+                x_quant(g - 1)
+            if 0 <= b < 8 and b % 2 == 1:
+                w_quant(b // 2)
+            if b - 2 >= 0 and (b - 2) % 2 == 1 and (b - 2) // 2 < 2:
+                mx((b - 2) // 2)
+            if 1 <= j < 9:
+                first_term(j - 1, nc.gpsimd)
+        nbank = 8
+        nquant = 4
+        for s in range(2, 20):
+            while nbank < 32 and nbank < 2 * (s + 3):
+                w_transposes(nbank)
+                w_transposes(nbank + 1)
+                w_copy(nbank)
+                w_copy(nbank + 1)
+                nbank += 2
+            if 4 <= s < 12:
+                gate_mm(s + 4)
+                gate_sig(s + 4)
+            while nquant < 16 and nquant <= s + 1:
+                w_quant(nquant)
+                nquant += 1
+            if s < 19:
+                mx(s)
+            if 5 <= s < 13:
+                first_term(s + 3, nc.vector)
+            if 3 <= s < 19:
+                second_term((s - 3) // NB, (s - 3) % NB)
+            if s >= 4:
+                finish((s - 4) // NB, (s - 4) % NB, nc.vector)

@@ -23,6 +23,7 @@ NCH = CO // CW
 FLOPS = 2 * NT * C * CO + 2 * NT * 128 * CO
 
 PINNED = True
+V0_BY_MATMUL = 11
 REG_ENG = "V"
 T1_ENG = "G"
 
@@ -48,6 +49,11 @@ def tile_full_tmix_params_pb_kernel(tc, x, x_v, W_v, v_hid, v2, v0, v_first, out
         make_identity(nc, ident_b[:])
         v0rows = const.tile([P, P], BF16, name="v0rows")
         nc.gpsimd.memset(v0rows[:], 0.0)
+        onesrow = const.tile([P, P], BF16, name="onesrow")
+        nc.vector.memset(onesrow[:], 0.0)
+        nc.vector.memset(onesrow[0:1, :], 1.0)
+        v0pad = const.tile([P, CO], BF16, name="v0pad")
+        nc.gpsimd.memset(v0pad[:], 0.0)
 
         a_bf = const.tile([P, 4, 4], BF16, name="a_bf")
         nc.scalar.dma_start(out=a_bf[:], in_=x_v.rearrange("a b c -> (a b c)").rearrange("(m p e) -> p m e", p=P, e=4))
@@ -79,6 +85,7 @@ def tile_full_tmix_params_pb_kernel(tc, x, x_v, W_v, v_hid, v2, v0, v_first, out
         load_x(0)
         nc.sync.dma_start(out=vh_sb[:], in_=v_hid.rearrange("b t d -> t b d"))
         nc.sync.dma_start(out=v0rows[0:16, :], in_=v0.rearrange("a b c -> (a b c)").rearrange("(j p) -> j p", p=P))
+        nc.sync.dma_start(out=v0pad[0:1, :], in_=v0.rearrange("a b c -> (a b) c"))
         nc.sync.dma_start(out=v2_sb[:], in_=v2)
         load_x(1)
         load_w(0)
@@ -175,10 +182,13 @@ def tile_full_tmix_params_pb_kernel(tc, x, x_v, W_v, v_hid, v2, v0, v_first, out
             hp = tp_pool.tile([P, CW], F32, name="hp", tag="tp")
             nc.tensor.matmul(out=hp[:], lhsT=vhT[:, P * i:P * i + P], rhs=v2_sb[:, CW * c:CW * c + CW],
                              start=True, stop=False)
-            for q in range(4):
-                jj = 4 * c + q
-                nc.tensor.matmul(out=hp[:, P * q:P * q + P], lhsT=v0c[:, jj:jj + 1].to_broadcast([P, P]),
-                                 rhs=ident_f[:], is_transpose=True, start=False, stop=(q == 3))
+            if k >= 16 - V0_BY_MATMUL:
+                nc.tensor.matmul(out=hp[:], lhsT=onesrow[:], rhs=v0pad[:, CW * c:CW * c + CW], start=False, stop=True)
+            else:
+                for q in range(4):
+                    jj = 4 * c + q
+                    nc.tensor.matmul(out=hp[:, P * q:P * q + P], lhsT=v0c[:, jj:jj + 1].to_broadcast([P, P]),
+                                     rhs=ident_f[:], is_transpose=True, start=False, stop=(q == 3))
             hps[k] = hp
 
         def gate_sig(k):

@@ -85,13 +85,13 @@ def tile_full_tmix_params_pb_kernel(tc, x, x_v, W_v, v_hid, v2, v0, v_first, out
         load_x(0)
         nc.sync.dma_start(out=vh_sb[:], in_=v_hid.rearrange("b t d -> t b d"))
         nc.sync.dma_start(out=v0rows[0:16, :], in_=v0.rearrange("a b c -> (a b c)").rearrange("(j p) -> j p", p=P))
-        nc.sync.dma_start(out=v0pad[0:1, :], in_=v0.rearrange("a b c -> (a b) c"))
         nc.sync.dma_start(out=v2_sb[:], in_=v2)
         load_x(1)
         load_w(0)
         load_w(1)
         load_x(2)
         load_x(3)
+        nc.sync.dma_start(out=v0pad[0:1, :], in_=v0.rearrange("a b c -> (a b) c"))
         load_vf(0)
         load_w(2)
         load_w(3)
@@ -296,7 +296,7 @@ def tile_full_tmix_params_pb_kernel(tc, x, x_v, W_v, v_hid, v2, v0, v_first, out
             if s < 19:
                 mx(s)
             if 5 <= s < 13:
-                first_term(s + 3, nc.vector)
+                first_term(s + 3, nc.gpsimd)
             if 3 <= s < 19:
                 second_term((s - 3) // NB, (s - 3) % NB)
             if s >= 4:

@@ -23,6 +23,7 @@ NCH = CO // CW
 FLOPS = 2 * NT * C * CO + 2 * NT * 128 * CO
 
 PINNED = True
+GPSIMD_FINISH = (11, 13)
 V0_BY_MATMUL = 11
 REG_ENG = "V"
 T1_ENG = "G"
@@ -35,7 +36,7 @@ def tile_full_tmix_params_pb_kernel(tc, x, x_v, W_v, v_hid, v2, v0, v_first, out
             ctx.enter_context(tc.manual_schedule())
         const = ctx.enter_context(tc.tile_pool(name="const", bufs=1))
         wraw_pool = ctx.enter_context(tc.tile_pool(name="wraw", bufs=6))
-        wg_pool = ctx.enter_context(tc.tile_pool(name="wg", bufs=3))
+        wg_pool = ctx.enter_context(tc.tile_pool(name="wg", bufs=4))
         wc_pool = ctx.enter_context(tc.tile_pool(name="wc", bufs=6))
         xw_pool = ctx.enter_context(tc.tile_pool(name="xw", bufs=2))
         vf_pool = ctx.enter_context(tc.tile_pool(name="vf", bufs=3))
@@ -126,7 +127,10 @@ def tile_full_tmix_params_pb_kernel(tc, x, x_v, W_v, v_hid, v2, v0, v_first, out
 
         def x_transposes(j):
             g, u = divmod(j, 2)
-            bank = tp_pool.tile([P, NT], F32, name="xbank", tag="tp")
+            if j < 4:
+                bank = acc_pool.tile([P, NT], F32, name="xbank", tag="acc")
+            else:
+                bank = tp_pool.tile([P, NT], F32, name="xbank", tag="tp")
             for b in range(NB):
                 nc.tensor.transpose(bank[:, P * b:P * b + P], xp[g][:, b, :].bitcast(F32)[:, u:2 * P:2], ident_f[:])
             xbanks[j] = bank
@@ -281,7 +285,7 @@ def tile_full_tmix_params_pb_kernel(tc, x, x_v, W_v, v_hid, v2, v0, v_first, out
         nbank = 8
         nquant = 4
         for s in range(2, 20):
-            while nbank < 32 and nbank < 2 * (s + 3):
+            while nbank < 32 and nbank < 2 * (s + 4):
                 w_transposes(nbank)
                 w_transposes(nbank + 1)
                 w_copy(nbank)
@@ -300,4 +304,4 @@ def tile_full_tmix_params_pb_kernel(tc, x, x_v, W_v, v_hid, v2, v0, v_first, out
             if 3 <= s < 19:
                 second_term((s - 3) // NB, (s - 3) % NB)
             if s >= 4:
-                finish((s - 4) // NB, (s - 4) % NB, nc.vector)
+                finish((s - 4) // NB, (s - 4) % NB, nc.gpsimd if (s - 4) in GPSIMD_FINISH else nc.vector)

@@ -300,7 +300,7 @@ def tile_full_tmix_params_pb_kernel(tc, x, x_v, W_v, v_hid, v2, v0, v_first, out
             if s < 19:
                 mx(s)
             if 5 <= s < 13:
-                first_term(s + 3, nc.gpsimd)
+                first_term(s + 3, nc.vector)
             if 3 <= s < 19:
                 second_term((s - 3) // NB, (s - 3) % NB)
             if s >= 4:

@@ -23,7 +23,7 @@ NCH = CO // CW
 FLOPS = 2 * NT * C * CO + 2 * NT * 128 * CO
 
 PINNED = True
-GPSIMD_FINISH = (11, 13)
+GPSIMD_FINISH = range(4, 12)
 V0_BY_MATMUL = 11
 REG_ENG = "V"
 T1_ENG = "G"
@@ -142,8 +142,12 @@ def tile_full_tmix_params_pb_kernel(tc, x, x_v, W_v, v_hid, v2, v0, v_first, out
             view = xbanks[j][:].bitcast(BF16).rearrange("p (s e) -> p s e", e=2)
             for e in range(2):
                 t = 2 * u + e
-                nc.scalar.activation(out=y0s[g][:, t, :], in_=view[:, :, e], func=ACT.Copy,
-                                     scale=oma32[:, 4 * g + t:4 * g + t + 1])
+                if j == 1 and e == 1:
+                    nc.vector.tensor_scalar(out=y0s[g][:, t, :], in0=view[:, :, e], scalar1=oma32[:, 4 * g + t:4 * g + t + 1],
+                                            scalar2=None, op0=ALU.mult)
+                else:
+                    nc.scalar.activation(out=y0s[g][:, t, :], in_=view[:, :, e], func=ACT.Copy,
+                                         scale=oma32[:, 4 * g + t:4 * g + t + 1])
 
         def x_add(j):
             g, u = divmod(j, 2)
@@ -157,11 +161,10 @@ def tile_full_tmix_params_pb_kernel(tc, x, x_v, W_v, v_hid, v2, v0, v_first, out
                 nc.vector.scalar_tensor_tensor(out=xvv[:, t, :, 1:P], in0=view[:, :, 0:P - 1, e],
                                                scalar=a32[:, 4 * g + t:4 * g + t + 1], in1=y0v[:, t, :, 1:P],
                                                op0=ALU.mult, op1=ALU.add)
+                if t == 2:
+                    nc.vector.tensor_copy(out=xvv[:, :, :, 0], in_=y0v[:, :, :, 0])
 
         def x_regroup(g):
-            y0v = y0s[g][:].rearrange("p t (b s) -> p t b s", b=NB)
-            xvv = xvps[g][:].rearrange("p t (b s) -> p t b s", b=NB)
-            nc.vector.tensor_copy(out=xvv[:, :, :, 0], in_=y0v[:, :, :, 0])
             xgs[g] = xw_pool.tile([P, NT * 4], BF16, name="xg", align_bytes=64)
             dst = xgs[g][:].rearrange("p (c i t) -> p c t i", i=4, t=4)
             src = xvps[g][:].rearrange("p t (c i) -> p c t i", i=4)
@@ -233,10 +236,13 @@ def tile_full_tmix_params_pb_kernel(tc, x, x_v, W_v, v_hid, v2, v0, v_first, out
         accs = {}
 
         def mx(s):
-            todo = sorted([((s - i) % NG, i) for i in range(NB) if 0 <= s - i < 16], reverse=True)
-            for g, i in todo:
-                c = (s - i) // NG
-                wc, ws = wcs[s - i]
+            if s < NG:
+                todo = [(s, i, s) for i in range(NB)]
+            else:
+                todo = sorted([((s - i) % NG, i, s - i) for i in range(NB) if NG <= s - i < 16], reverse=True)
+            for g, i, slot in todo:
+                c = slot // NG
+                wc, ws = wcs[slot]
                 if g == 0:
                     accs[(c, i)] = acc_pool.tile([P, CW], F32, name="acc", tag="acc")
                 nc.tensor.matmul_mx(out=accs[(c, i)][:],
@@ -272,15 +278,15 @@ def tile_full_tmix_params_pb_kernel(tc, x, x_v, W_v, v_hid, v2, v0, v_first, out
                 x_transposes(j + 1)
             if 0 <= b < 8:
                 w_copy(b)
-            if j < 8 and u == 1:
-                x_regroup(g)
             if u == 0 and 1 <= g <= 4:
+                x_regroup(g - 1)
+            if u == 1 and 1 <= g <= 4:
                 x_quant(g - 1)
             if 0 <= b < 8 and b % 2 == 1:
                 w_quant(b // 2)
             if b - 2 >= 0 and (b - 2) % 2 == 1 and (b - 2) // 2 < 2:
                 mx((b - 2) // 2)
-            if 1 <= j < 9:
+            if 1 <= j < 9 and (True):
                 first_term(j - 1, nc.gpsimd)
         nbank = 8
         nquant = 4
@@ -299,9 +305,17 @@ def tile_full_tmix_params_pb_kernel(tc, x, x_v, W_v, v_hid, v2, v0, v_first, out
                 nquant += 1
             if s < 19:
                 mx(s)
-            if 5 <= s < 13:
-                first_term(s + 3, nc.vector)
-            if 3 <= s < 19:
+            for k in range(16):
+                j = k + 1
+                if s == (2 + k // 4 if k < 8 else k - 3) and (k >= 8 or not (True)):
+                    first_term(k, nc.vector)
+            if s == 3:
+                for i in range(NB):
+                    second_term(0, i)
+            if s == 4:
+                for i in range(NB):
+                    finish(0, i, nc.vector)
+            if 7 <= s < 19:
                 second_term((s - 3) // NB, (s - 3) % NB)
-            if s >= 4:
+            if s >= 8:
                 finish((s - 4) // NB, (s - 4) % NB, nc.gpsimd if (s - 4) in GPSIMD_FINISH else nc.vector)

@@ -23,7 +23,7 @@ NCH = CO // CW
 FLOPS = 2 * NT * C * CO + 2 * NT * 128 * CO
 
 PINNED = True
-GPSIMD_FINISH = range(4, 12)
+GPSIMD_FINISH = (4, 5, 6, 7, 8, 9, 11, 13)
 V0_BY_MATMUL = 11
 REG_ENG = "V"
 T1_ENG = "G"
@@ -89,14 +89,14 @@ def tile_full_tmix_params_pb_kernel(tc, x, x_v, W_v, v_hid, v2, v0, v_first, out
         nc.sync.dma_start(out=v2_sb[:], in_=v2)
         load_x(1)
         load_w(0)
+        load_vf(0)
         load_w(1)
         load_x(2)
         load_x(3)
         nc.sync.dma_start(out=v0pad[0:1, :], in_=v0.rearrange("a b c -> (a b) c"))
-        load_vf(0)
+        load_vf(1)
         load_w(2)
         load_w(3)
-        load_vf(1)
         load_w(4)
         load_w(5)
         load_vf(2)

@@ -37,7 +37,7 @@ def tile_full_tmix_params_pb_kernel(tc, x, x_v, W_v, v_hid, v2, v0, v_first, out
         const = ctx.enter_context(tc.tile_pool(name="const", bufs=1))
         wraw_pool = ctx.enter_context(tc.tile_pool(name="wraw", bufs=6))
         wg_pool = ctx.enter_context(tc.tile_pool(name="wg", bufs=4))
-        wc_pool = ctx.enter_context(tc.tile_pool(name="wc", bufs=6))
+        wc_pool = ctx.enter_context(tc.tile_pool(name="wc", bufs=7))
         xw_pool = ctx.enter_context(tc.tile_pool(name="xw", bufs=2))
         vf_pool = ctx.enter_context(tc.tile_pool(name="vf", bufs=3))
         p_pool = ctx.enter_context(tc.tile_pool(name="pp", bufs=4))
@@ -262,6 +262,7 @@ def tile_full_tmix_params_pb_kernel(tc, x, x_v, W_v, v_hid, v2, v0, v_first, out
             eng.tensor_tensor(out=t1[(c, i)][:], in0=t1[(c, i)][:], in1=pts[(c, i)][:], op=ALU.subtract)
             nc.sync.dma_start(out=out[i, :, CW * c:CW * c + CW], in_=t1[(c, i)][:])
 
+        head_gates = ((0,), (1,), (2,), (3,), (4,), (5,), (6,), (7,))
         x_transposes(0)
         gate_setup()
         for j in range(10):
@@ -269,9 +270,11 @@ def tile_full_tmix_params_pb_kernel(tc, x, x_v, W_v, v_hid, v2, v0, v_first, out
             b = j - 2
             if j < 8:
                 x_scale(j)
-                gate_mm(j)
+                for k in head_gates[j]:
+                    gate_mm(k)
                 x_add(j)
-                gate_sig(j)
+                for k in head_gates[j]:
+                    gate_sig(k)
             if 0 <= b < 8:
                 w_transposes(b)
             if j < 7:
@@ -297,10 +300,10 @@ def tile_full_tmix_params_pb_kernel(tc, x, x_v, W_v, v_hid, v2, v0, v_first, out
                 w_copy(nbank)
                 w_copy(nbank + 1)
                 nbank += 2
-            if 4 <= s < 12:
-                gate_mm(s + 4)
-                gate_sig(s + 4)
-            while nquant < 16 and nquant <= s + 1:
+            if 3 <= s < 11:
+                gate_mm(s + 5)
+                gate_sig(s + 5)
+            while nquant < 16 and nquant <= s + 2:
                 w_quant(nquant)
                 nquant += 1
             if s < 19:

from contextlib import ExitStack

import concourse.mybir as mybir
from concourse.masks import make_identity

F32 = mybir.dt.float32
BF16 = mybir.dt.bfloat16
U32 = mybir.dt.uint32
U8 = mybir.dt.uint8
FP8X4 = mybir.dt.float8_e4m3fn_x4
ALU = mybir.AluOpType
ACT = mybir.ActivationFunctionType

P = 128
NB = 4
NT = NB * P
C = 2048
CO = 2048
NG = 4
CW = 512
NCH = CO // CW

FLOPS = 2 * NT * C * CO + 2 * NT * 128 * CO

PINNED = True
GPSIMD_FINISH = (4, 5, 6, 7, 8, 9, 11, 13)
V0_BY_MATMUL = 11
REG_ENG = "V"
T1_ENG = "G"


def tile_full_tmix_params_pb_kernel(tc, x, x_v, W_v, v_hid, v2, v0, v_first, out):
    nc = tc.nc
    with ExitStack() as ctx:
        if PINNED:
            ctx.enter_context(tc.manual_schedule())
        const = ctx.enter_context(tc.tile_pool(name="const", bufs=1))
        wraw_pool = ctx.enter_context(tc.tile_pool(name="wraw", bufs=6))
        wg_pool = ctx.enter_context(tc.tile_pool(name="wg", bufs=4))
        wc_pool = ctx.enter_context(tc.tile_pool(name="wc", bufs=7))
        xw_pool = ctx.enter_context(tc.tile_pool(name="xw", bufs=2))
        vf_pool = ctx.enter_context(tc.tile_pool(name="vf", bufs=3))
        p_pool = ctx.enter_context(tc.tile_pool(name="pp", bufs=4))
        acc_pool = ctx.enter_context(tc.psum_pool(name="acc", bufs=4))
        tp_pool = ctx.enter_context(tc.psum_pool(name="tp", bufs=4))

        ident_f = const.tile([P, P], F32, name="ident_f")
        make_identity(nc, ident_f[:])
        ident_b = const.tile([P, P], BF16, name="ident_b")
        make_identity(nc, ident_b[:])
        v0rows = const.tile([P, P], BF16, name="v0rows")
        nc.gpsimd.memset(v0rows[:], 0.0)
        onesrow = const.tile([P, P], BF16, name="onesrow")
        nc.vector.memset(onesrow[:], 0.0)
        nc.vector.memset(onesrow[0:1, :], 1.0)
        v0pad = const.tile([P, CO], BF16, name="v0pad")
        nc.gpsimd.memset(v0pad[:], 0.0)

        a_bf = const.tile([P, 4, 4], BF16, name="a_bf")
        nc.scalar.dma_start(out=a_bf[:], in_=x_v.rearrange("a b c -> (a b c)").rearrange("(m p e) -> p m e", p=P, e=4))

        warm = const.tile([P, 1], F32, name="warm")
        nc.vector.memset(warm[:], 0.0)
        nc.scalar.activation(out=warm[:], in_=warm[:], func=ACT.Sigmoid)

        x_tbk = x.rearrange("b t k -> t b k")
        w_units = W_v.rearrange("(n r p) k -> n p r k", r=2, p=P)
        vf_chunks = v_first.rearrange("b t (c n) -> c t b n", n=CW)
        xp = [const.tile([P, NB, C // NG], BF16, name="xp%d" % g) for g in range(NG)]
        vh_sb = const.tile([P, NB, P], BF16, name="vh_sb")
        v2_sb = const.tile([P, CO], BF16, name="v2_sb")
        wraw = {}
        vf_sb = {}

        def load_w(n):
            wraw[n] = wraw_pool.tile([P, 2, C], BF16, name="wr")
            nc.sync.dma_start(out=wraw[n][:], in_=w_units[n])

        def load_vf(c):
            vf_sb[c] = vf_pool.tile([P, NB, CW], BF16, name="vf")
            nc.sync.dma_start(out=vf_sb[c][:], in_=vf_chunks[c])

        def load_x(g):
            nc.sync.dma_start(out=xp[g][:], in_=x_tbk[:, :, 512 * g:512 * g + 512])

        load_x(0)
        nc.sync.dma_start(out=vh_sb[:], in_=v_hid.rearrange("b t d -> t b d"))
        nc.sync.dma_start(out=v0rows[0:16, :], in_=v0.rearrange("a b c -> (a b c)").rearrange("(j p) -> j p", p=P))
        nc.sync.dma_start(out=v2_sb[:], in_=v2)
        load_x(1)
        load_w(0)
        load_vf(0)
        load_w(1)
        load_x(2)
        load_x(3)
        nc.sync.dma_start(out=v0pad[0:1, :], in_=v0.rearrange("a b c -> (a b) c"))
        load_vf(1)
        load_w(2)
        load_w(3)
        load_w(4)
        load_w(5)
        load_vf(2)
        load_vf(3)
        load_w(6)
        load_w(7)

        a32 = const.tile([P, 16], F32, name="a32")
        nc.vector.tensor_copy(out=a32[:], in_=a_bf[:].rearrange("p m e -> p (m e)"))
        oma32 = const.tile([P, 16], F32, name="oma32")
        nc.vector.tensor_scalar(out=oma32[:], in0=a32[:], scalar1=-1.0, scalar2=1.0, op0=ALU.mult, op1=ALU.add)

        xcodes = const.tile([P, NG, NT], U32, name="xcodes", align_bytes=64)
        xscales = const.tile([P, NG, NT], U8, name="xscales", align_bytes=64)
        mix = {}
        t1 = {}
        for c in range(NCH):
            for i in range(NB):
                mix[(c, i)] = const.tile([P, CW], F32, name="mix%d_%d" % (c, i))
                t1[(c, i)] = const.tile([P, CW], F32, name="t1_%d_%d" % (c, i))
        vhT = const.tile([P, NT], BF16, name="vhT")
        v0c = const.tile([P, 16], F32, name="v0c")

        xbanks = {}
        y0s = {}
        xvps = {}
        xgs = {}

        def x_transposes(j):
            g, u = divmod(j, 2)
            if j < 4:
                bank = acc_pool.tile([P, NT], F32, name="xbank", tag="acc")
            else:
                bank = tp_pool.tile([P, NT], F32, name="xbank", tag="tp")
            for b in range(NB):
                nc.tensor.transpose(bank[:, P * b:P * b + P], xp[g][:, b, :].bitcast(F32)[:, u:2 * P:2], ident_f[:])
            xbanks[j] = bank

        def x_scale(j):
            g, u = divmod(j, 2)
            if u == 0:
                y0s[g] = xw_pool.tile([P, 4, NT], F32, name="y0")
            view = xbanks[j][:].bitcast(BF16).rearrange("p (s e) -> p s e", e=2)
            for e in range(2):
                t = 2 * u + e
                if j == 1 and e == 1:
                    nc.vector.tensor_scalar(out=y0s[g][:, t, :], in0=view[:, :, e], scalar1=oma32[:, 4 * g + t:4 * g + t + 1],
                                            scalar2=None, op0=ALU.mult)
                else:
                    nc.scalar.activation(out=y0s[g][:, t, :], in_=view[:, :, e], func=ACT.Copy,
                                         scale=oma32[:, 4 * g + t:4 * g + t + 1])

        def x_add(j):
            g, u = divmod(j, 2)
            if u == 0:
                xvps[g] = xw_pool.tile([P, 4, NT], BF16, name="xvp")
            y0v = y0s[g][:].rearrange("p t (b s) -> p t b s", b=NB)
            xvv = xvps[g][:].rearrange("p t (b s) -> p t b s", b=NB)
            view = xbanks[j][:].bitcast(BF16).rearrange("p (b s e) -> p b s e", b=NB, e=2)
            for e in range(2):
                t = 2 * u + e
                nc.vector.scalar_tensor_tensor(out=xvv[:, t, :, 1:P], in0=view[:, :, 0:P - 1, e],
                                               scalar=a32[:, 4 * g + t:4 * g + t + 1], in1=y0v[:, t, :, 1:P],
                                               op0=ALU.mult, op1=ALU.add)
                if t == 2:
                    nc.vector.tensor_copy(out=xvv[:, :, :, 0], in_=y0v[:, :, :, 0])

        def x_regroup(g):
            xgs[g] = xw_pool.tile([P, NT * 4], BF16, name="xg", align_bytes=64)
            dst = xgs[g][:].rearrange("p (c i t) -> p c t i", i=4, t=4)
            src = xvps[g][:].rearrange("p t (c i) -> p c t i", i=4)
            nc.vector.tensor_copy(out=dst, in_=src)

        def x_quant(g):
            nc.vector.quantize_mx(out=xcodes[:, g, :].bitcast(FP8X4), scales=xscales[:, g, :], in_=xgs[g][:])

        def gate_setup():
            bank = tp_pool.tile([P, NT], BF16, name="vhbank", tag="tp")
            for b in range(NB):
                nc.tensor.transpose(bank[:, P * b:P * b + P], vh_sb[:, b, :], ident_b[:])
            nc.scalar.copy(out=vhT[:], in_=bank[:])
            vbank = tp_pool.tile([P, P], BF16, name="vbank", tag="tp")
            nc.tensor.transpose(vbank[:], v0rows[:], ident_b[:])
            nc.vector.tensor_copy(out=v0c[:], in_=vbank[:, 0:16])

        hps = {}

        def gate_mm(k):
            c, i = divmod(k, NB)
            hp = tp_pool.tile([P, CW], F32, name="hp", tag="tp")
            nc.tensor.matmul(out=hp[:], lhsT=vhT[:, P * i:P * i + P], rhs=v2_sb[:, CW * c:CW * c + CW],
                             start=True, stop=False)
            if k >= 16 - V0_BY_MATMUL:
                nc.tensor.matmul(out=hp[:], lhsT=onesrow[:], rhs=v0pad[:, CW * c:CW * c + CW], start=False, stop=True)
            else:
                for q in range(4):
                    jj = 4 * c + q
                    nc.tensor.matmul(out=hp[:, P * q:P * q + P], lhsT=v0c[:, jj:jj + 1].to_broadcast([P, P]),
                                     rhs=ident_f[:], is_transpose=True, start=False, stop=(q == 3))
            hps[k] = hp

        def gate_sig(k):
            nc.scalar.activation(out=mix[divmod(k, NB)][:], in_=hps[k][:], func=ACT.Sigmoid)

        def first_term(k, eng):
            c, i = divmod(k, NB)
            eng.tensor_tensor(out=t1[(c, i)][:], in0=vf_sb[c][:, i, :], in1=mix[(c, i)][:], op=ALU.mult)

        wbanks = {}
        wgs = {}
        wcs = {}

        def w_transposes(b):
            c, rest = divmod(b, 8)
            g, h = divmod(rest, 2)
            bank = tp_pool.tile([P, 512], F32, name="wbank", tag="tp")
            for u in range(2):
                for r in range(2):
                    lo = 256 * g + u
                    nc.tensor.transpose(bank[:, 256 * u + P * r:256 * u + P * r + P],
                                        wraw[2 * c + h][:, r, :].bitcast(F32)[:, lo:256 * g + 256:2], ident_f[:])
            wbanks[b] = bank

        def w_copy(b):
            k, h = divmod(b, 2)
            if h == 0:
                wgs[k] = wg_pool.tile([P, CW * 4], BF16, name="wg", align_bytes=64)
            nc.scalar.copy(out=wgs[k][:].bitcast(F32)[:, 512 * h:512 * h + 512].rearrange("p (c u) -> p c u", u=2),
                           in_=wbanks[b][:].rearrange("p (u c) -> p c u", u=2))

        def w_quant(k):
            wc = wc_pool.tile([P, CW], U32, name="wc", align_bytes=64)
            ws = wc_pool.tile([P, CW], U8, name="ws", align_bytes=64)
            nc.vector.quantize_mx(out=wc[:].bitcast(FP8X4), scales=ws[:], in_=wgs[k][:])
            wcs[k] = (wc, ws)

        accs = {}

        def mx(s):
            if s < NG:
                todo = [(s, i, s) for i in range(NB)]
            else:
                todo = sorted([((s - i) % NG, i, s - i) for i in range(NB) if NG <= s - i < 16], reverse=True)
            for g, i, slot in todo:
                c = slot // NG
                wc, ws = wcs[slot]
                if g == 0:
                    accs[(c, i)] = acc_pool.tile([P, CW], F32, name="acc", tag="acc")
                nc.tensor.matmul_mx(out=accs[(c, i)][:],
                                    lhsT=xcodes[:, g, P * i:P * i + P].bitcast(FP8X4),
                                    lhsT_scale=xscales[:, g, P * i:P * i + P],
                                    rhs=wc[:].bitcast(FP8X4), rhs_scale=ws[:],
                                    start=(g == 0), stop=(g == NG - 1))

        pts = {}

        def second_term(c, i):
            pts[(c, i)] = p_pool.tile([P, CW], F32, name="pt")
            nc.vector.scalar_tensor_tensor(out=pts[(c, i)][:], in0=mix[(c, i)][:], scalar=1.0, in1=accs[(c, i)][:],
                                           op0=ALU.subtract, op1=ALU.mult)

        def finish(c, i, eng):
            eng.tensor_tensor(out=t1[(c, i)][:], in0=t1[(c, i)][:], in1=pts[(c, i)][:], op=ALU.subtract)
            nc.sync.dma_start(out=out[i, :, CW * c:CW * c + CW], in_=t1[(c, i)][:])

        head_gates = ((0,), (1,), (2,), (3,), (4,), (5,), (6,), (7,))
        x_transposes(0)
        gate_setup()
        for j in range(10):
            g, u = divmod(j, 2)
            b = j - 2
            if j < 8:
                x_scale(j)
                for k in head_gates[j]:
                    gate_mm(k)
                x_add(j)
                for k in head_gates[j]:
                    gate_sig(k)
            if 0 <= b < 8:
                w_transposes(b)
            if j < 7:
                x_transposes(j + 1)
            if 0 <= b < 8:
                w_copy(b)
            if u == 0 and 1 <= g <= 4:
                x_regroup(g - 1)
            if u == 1 and 1 <= g <= 4:
                x_quant(g - 1)
            if 0 <= b < 8 and b % 2 == 1:
                w_quant(b // 2)
            if b - 2 >= 0 and (b - 2) % 2 == 1 and (b - 2) // 2 < 2:
                mx((b - 2) // 2)
            if 1 <= j < 9 and (True):
                first_term(j - 1, nc.gpsimd)
        nbank = 8
        nquant = 4
        for s in range(2, 20):
            while nbank < 32 and nbank < 2 * (s + 4):
                w_transposes(nbank)
                w_transposes(nbank + 1)
                w_copy(nbank)
                w_copy(nbank + 1)
                nbank += 2
            if 3 <= s < 11:
                gate_mm(s + 5)
                gate_sig(s + 5)
            while nquant < 16 and nquant <= s + 2:
                w_quant(nquant)
                nquant += 1
            if s < 19:
                mx(s)
            for k in range(16):
                j = k + 1
                if s == (2 + k // 4 if k < 8 else k - 3) and (k >= 8 or not (True)):
                    first_term(k, nc.vector)
            if s == 3:
                for i in range(NB):
                    second_term(0, i)
            if s == 4:
                for i in range(NB):
                    finish(0, i, nc.vector)
            if 7 <= s < 19:
                second_term((s - 3) // NB, (s - 3) % NB)
            if s >= 8:
                finish((s - 4) // NB, (s - 4) % NB, nc.gpsimd if (s - 4) in GPSIMD_FINISH else nc.vector)
